import numpy as np
import ml_dtypes


def mxq(x, axis, fmt="e4m3"):
    dtype, down = {"e4m3": (ml_dtypes.float8_e4m3fn, 7), "e5m2": (ml_dtypes.float8_e5m2, 14)}[fmt]
    v = np.moveaxis(np.asarray(x, np.float32).astype(ml_dtypes.bfloat16).astype(np.float64), axis, -1)
    blocks = v.reshape(v.shape[:-1] + (-1, 32))
    amax = np.abs(blocks).max(-1, keepdims=True)
    byte = np.maximum(np.where(amax > 0, np.frexp(amax)[1] - 1 + 127, 0) - down, 1)
    scale = np.exp2(byte - 127.0)
    codes = (blocks / scale).astype(np.float32).astype(dtype).astype(np.float64)
    return np.moveaxis((codes * scale).reshape(v.shape), -1, axis)


WIDE = False


def mx_kscale(k):
    if not WIDE:
        return np.ones(k)
    levels = np.array([10, -10, 5, -5, 0])
    a = np.random.permutation(np.resize(levels, k // 512 * 4)).reshape(k // 512, 4)
    idx = np.arange(k)
    return np.exp2(a[idx // 512, idx % 128 // 32])


BF16 = ml_dtypes.bfloat16


def bf(x):
    return np.asarray(x, np.float32).astype(BF16)


def f64(x):
    return np.asarray(x).astype(np.float64)


B, T, DM, DH, L = 4, 512, 1024, 1024, 512


def sigmoid(x):
    return 1.0 / (1.0 + np.exp(-x))


def setup_inputs():
    s, t = mx_kscale(DM), mx_kscale(DH)
    return {"q": bf(np.random.standard_normal((B, T, DM)) * s),
            "num": bf(np.random.standard_normal((B, T, DH)) * 1.9 * np.sqrt(T) * t),
            "den": bf(0.5 * T * (0.5 + np.random.random((B, T, DH)))),
            "Wq": bf(np.random.standard_normal((DH, DM)) / np.sqrt(DM) / s),
            "Wo": bf(np.random.standard_normal((DM, DH)) * 5.0 / np.sqrt(DH) / t)}


def reference(q, num, den, Wq, Wo):
    Q = mxq(f64(q), 2, "e4m3") @ mxq(f64(Wq), 1, "e4m3").T
    Yt = sigmoid(Q) * f64(num) / f64(den)
    return mxq(Yt, 2, "e4m3") @ mxq(f64(Wo), 1, "e4m3").T

@@ -1,0 +1,210 @@
+from contextlib import ExitStack
+
+import concourse.mybir as mybir
+from concourse.masks import make_identity
+
+F32 = mybir.dt.float32
+BF16 = mybir.dt.bfloat16
+U32 = mybir.dt.uint32
+U8 = mybir.dt.uint8
+FP8X4 = mybir.dt.float8_e4m3fn_x4
+ACT = mybir.ActivationFunctionType
+MULT = mybir.AluOpType.mult
+
+P = 128
+PACK = 4
+K_PASS = P * PACK
+WIDTH = 1024
+PASSES = WIDTH // K_PASS
+BLOCK = 512
+ROW_TILES = BLOCK // P
+PAIR = 2 * P
+TOKENS = 2048
+CHUNKS = TOKENS // BLOCK
+UNITS = CHUNKS * PASSES
+PROJECT_BEHIND = 3
+RATIO_AHEAD = 4
+
+FLOPS = 2 * 2 * TOKENS * WIDTH * WIDTH
+
+
+def tile_aftfull_pb_kernel(tc, q, num, den, Wq, Wo, out):
+    nc = tc.nc
+
+    by_token = "(n p i) k -> n p (i k)"
+    q_rows = q.flatten_outer_dims().rearrange(by_token, p=P, i=ROW_TILES).unsqueeze(2)
+    num_rows = num.flatten_outer_dims().rearrange(by_token, p=P, i=ROW_TILES).unsqueeze(2)
+    den_rows = den.flatten_outer_dims().rearrange(by_token, p=P, i=ROW_TILES).unsqueeze(2)
+    out_rows = out.flatten_outer_dims().rearrange("(n p i) o -> n p i o", p=P, i=ROW_TILES)
+    wq_rows = Wq.rearrange("(g u p e) k -> g p u (e k)", u=2, p=P, e=2)
+    wo_rows = Wo.rearrange("(s i p) h -> s p i h", i=ROW_TILES, p=P)
+
+    with ExitStack() as ctx:
+        ctx.enter_context(tc.manual_schedule())
+        const = ctx.enter_context(tc.tile_pool(name="const", bufs=1))
+        nat_pool = ctx.enter_context(tc.tile_pool(name="nat", bufs=5))
+        grouped_pool = ctx.enter_context(tc.tile_pool(name="grouped", bufs=2))
+        keep = ctx.enter_context(tc.tile_pool(name="keep", bufs=1))
+        sig_pool = ctx.enter_context(tc.tile_pool(name="sig", bufs=3))
+        y_pool = ctx.enter_context(tc.tile_pool(name="y", bufs=2))
+        out_pool = ctx.enter_context(tc.tile_pool(name="outs", bufs=4))
+        work = ctx.enter_context(tc.psum_pool(name="work", bufs=4))
+        gate_pool = ctx.enter_context(tc.psum_pool(name="gate", bufs=4))
+
+        ident = const.tile([P, P], F32, name="ident")
+        make_identity(nc, ident[:])
+
+        def load(rows):
+            nat = nat_pool.tile([P, ROW_TILES, WIDTH], BF16, name="nat")
+            runs = rows.shape[1]
+            nc.sync.dma_start(out=nat[:].rearrange("p (a b) k -> p a (b k)", a=runs), in_=rows)
+            return nat
+
+        def mx_tiles(name):
+            return {
+                "codes": keep.tile([P, PASSES * BLOCK], U32, name=name + "_codes", align_bytes=64),
+                "scales": keep.tile([P, PASSES * BLOCK], U8, name=name + "_scales", align_bytes=64),
+            }
+
+        def turn(nat, c, pair):
+            words = nat[:].bitcast(F32)
+            bank = work.tile([P, 2, PAIR], F32, name="bank")
+            for u in range(2):
+                for h in range(2):
+                    block = 2 * c + u
+                    nc.tensor.transpose(
+                        out=bank[:, u, h * P : (h + 1) * P],
+                        in_=words[:, 2 * pair + h, block * P : (block + 1) * P],
+                        identity=ident[:],
+                    )
+            return bank
+
+        def as_values(bank):
+            return bank[:].bitcast(BF16).rearrange("p u (r e) -> p r u e", e=2)
+
+        def part_of(unit_tile, pair):
+            rows = unit_tile[:, pair * PAIR : (pair + 1) * PAIR, :]
+            return rows.rearrange("p r (u e) -> p r u e", e=2)
+
+        def regroup(nat, grouped, c, pair):
+            bank = turn(nat, c, pair)
+            nc.vector.tensor_copy(
+                out=grouped[:].bitcast(F32)[:, c, pair * PAIR : (pair + 1) * PAIR, :],
+                in_=bank[:].rearrange("p u r -> p r u"),
+            )
+
+        def quantise(grouped, operand):
+            nc.vector.quantize_mx(
+                out=operand["codes"][:].bitcast(FP8X4),
+                scales=operand["scales"][:],
+                in_=grouped[:].rearrange("p c r t -> p (c r t)"),
+            )
+
+        def log_denominator(nat, n, g, pair):
+            bank = turn(nat, g, pair)
+            nc.scalar.activation(out=part_of(ratio[PASSES * n + g], pair), in_=as_values(bank), func=ACT.Ln)
+
+        def ratio_unit(u):
+            n, g = divmod(u, PASSES)
+            for pair in range(2):
+                bank = turn(num_nat[n], g, pair)
+                part = part_of(ratio[u], pair)
+                nc.vector.tensor_tensor(out=part, in0=as_values(bank), in1=part, op=MULT)
+
+        def mx_product(acc, stationary, s_col, moving, m_col):
+            for c in range(PASSES):
+                s_cols = slice(c * BLOCK + s_col, c * BLOCK + s_col + P)
+                m_cols = slice(c * BLOCK + m_col, c * BLOCK + m_col + BLOCK)
+                nc.tensor.matmul_mx(
+                    out=acc[:],
+                    lhsT=stationary["codes"][:, s_cols].bitcast(FP8X4),
+                    lhsT_scale=stationary["scales"][:, s_cols],
+                    rhs=moving["codes"][:, m_cols].bitcast(FP8X4),
+                    rhs_scale=moving["scales"][:, m_cols],
+                    start=(c == 0),
+                    stop=(c == PASSES - 1),
+                )
+
+        def gate(u):
+            n, g = divmod(u, PASSES)
+            sig = sig_pool.tile([P, PACK, BLOCK], F32, name="sig")
+            for t in range(PACK):
+                acc = gate_pool.tile([P, BLOCK], F32, name="acc")
+                mx_product(acc, wq[g], t * P, qx[n], 0)
+                nc.scalar.activation(out=sig[:, t, :], in_=acc[:], func=ACT.Sigmoid)
+            return sig
+
+        def blend(u, sig):
+            y = y_pool.tile([P, BLOCK, PACK], BF16, name="y", align_bytes=64)
+            nc.vector.tensor_tensor(out=y[:], in0=sig[:].rearrange("p t r -> p r t"), in1=ratio[u][:], op=MULT)
+            return y
+
+        def quantise_y(u, y):
+            n, g = divmod(u, PASSES)
+            cols = slice(g * BLOCK, (g + 1) * BLOCK)
+            nc.vector.quantize_mx(
+                out=yx[n]["codes"][:, cols].bitcast(FP8X4),
+                scales=yx[n]["scales"][:, cols],
+                in_=y[:].rearrange("p r t -> p (r t)"),
+            )
+
+        def project(v):
+            n, half = divmod(v, 2)
+            for i in (2 * half, 2 * half + 1):
+                result = out_pool.tile([P, WIDTH], F32, name="result")
+                for s in range(2):
+                    acc = work.tile([P, BLOCK], F32, name="bank")
+                    mx_product(acc, yx[n], i * P, wo[s], 0)
+                    cols = slice(s * BLOCK, (s + 1) * BLOCK)
+                    if i % 2 == 1 and s == 1:
+                        nc.vector.tensor_copy(out=result[:, cols], in_=acc[:])
+                    else:
+                        nc.scalar.copy(out=result[:, cols], in_=acc[:])
+                nc.sync.dma_start(out=out_rows[n][:, i, :], in_=result[:])
+
+        den_nat = {}
+        mx_nat = {}
+        mx_rows = [wq_rows[0], wq_rows[1]] + [q_rows[n] for n in range(CHUNKS)] + [wo_rows[0], wo_rows[1]]
+        for k in range(CHUNKS):
+            den_nat[k] = load(den_rows[k])
+            mx_nat[k] = load(mx_rows[k])
+        for k in range(CHUNKS, len(mx_rows)):
+            mx_nat[k] = load(mx_rows[k])
+        num_nat = [load(num_rows[n]) for n in range(CHUNKS)]
+
+        wq = [mx_tiles("wq%d" % g) for g in range(PASSES)]
+        qx = [mx_tiles("q%d" % n) for n in range(CHUNKS)]
+        wo = [mx_tiles("wo%d" % s) for s in range(2)]
+        yx = [mx_tiles("y%d" % n) for n in range(CHUNKS)]
+        operands = wq + qx + wo
+        ratio = [keep.tile([P, BLOCK, PACK], F32, name="ratio%d" % u) for u in range(UNITS)]
+
+        grouped = {}
+        for k in range(len(operands)):
+            grouped[k] = grouped_pool.tile([P, PASSES, BLOCK, PACK], BF16, name="grouped", align_bytes=64)
+            for c in range(PASSES):
+                for pair in range(2):
+                    if k < CHUNKS:
+                        log_denominator(den_nat[k], k, c, pair)
+                    regroup(mx_nat[k], grouped[k], c, pair)
+            if k > 0:
+                quantise(grouped[k - 1], operands[k - 1])
+        quantise(grouped[len(operands) - 1], operands[len(operands) - 1])
+        for u in range(UNITS):
+            nc.scalar.activation(out=ratio[u][:], in_=ratio[u][:], func=ACT.Exp, scale=-1.0)
+
+        sig = {0: gate(0)}
+        y = {}
+        for u in range(RATIO_AHEAD):
+            ratio_unit(u)
+        for r in range(UNITS + PROJECT_BEHIND):
+            if r >= PROJECT_BEHIND:
+                project(r - PROJECT_BEHIND)
+            if r + 1 < UNITS:
+                sig[r + 1] = gate(r + 1)
+            if 1 <= r <= UNITS:
+                quantise_y(r - 1, y[r - 1])
+            if r < UNITS:
+                y[r] = blend(r, sig[r])
+            if r + RATIO_AHEAD < UNITS:
+                ratio_unit(r + RATIO_AHEAD)

@@ -17,13 +17,14 @@ K_PASS = P * PACK
 WIDTH = 1024
 PASSES = WIDTH // K_PASS
 BLOCK = 512
-ROW_TILES = BLOCK // P
 PAIR = 2 * P
+HALVES = BLOCK // PAIR
 TOKENS = 2048
 CHUNKS = TOKENS // BLOCK
 UNITS = CHUNKS * PASSES
+EARLY_CHUNKS = 2
 PROJECT_BEHIND = 3
-RATIO_AHEAD = 4
+RATIO_AHEAD = 7
 
 FLOPS = 2 * 2 * TOKENS * WIDTH * WIDTH
 
@@ -31,34 +32,37 @@ FLOPS = 2 * 2 * TOKENS * WIDTH * WIDTH
 def tile_aftfull_pb_kernel(tc, q, num, den, Wq, Wo, out):
     nc = tc.nc
 
-    by_token = "(n p i) k -> n p (i k)"
-    q_rows = q.flatten_outer_dims().rearrange(by_token, p=P, i=ROW_TILES).unsqueeze(2)
-    num_rows = num.flatten_outer_dims().rearrange(by_token, p=P, i=ROW_TILES).unsqueeze(2)
-    den_rows = den.flatten_outer_dims().rearrange(by_token, p=P, i=ROW_TILES).unsqueeze(2)
-    out_rows = out.flatten_outer_dims().rearrange("(n p i) o -> n p i o", p=P, i=ROW_TILES)
-    wq_rows = Wq.rearrange("(g u p e) k -> g p u (e k)", u=2, p=P, e=2)
-    wo_rows = Wo.rearrange("(s i p) h -> s p i h", i=ROW_TILES, p=P)
+    by_token = "(n p h j) k -> n h p (j k)"
+    q_rows = q.flatten_outer_dims().rearrange(by_token, p=P, h=HALVES, j=2).unsqueeze(3)
+    num_rows = num.flatten_outer_dims().rearrange(by_token, p=P, h=HALVES, j=2).unsqueeze(3)
+    den_rows = den.flatten_outer_dims().rearrange(by_token, p=P, h=HALVES, j=2).unsqueeze(3)
+    out_rows = out.flatten_outer_dims().rearrange("(n p i) o -> n p i o", p=P, i=2 * HALVES)
+    wq_rows = Wq.rearrange("(g u p e) k -> g u p (e k)", u=HALVES, p=P, e=2).unsqueeze(3)
+    wo_rows = Wo.rearrange("(s h j p) k -> s h p j k", h=HALVES, j=2, p=P)
 
     with ExitStack() as ctx:
         ctx.enter_context(tc.manual_schedule())
         const = ctx.enter_context(tc.tile_pool(name="const", bufs=1))
-        nat_pool = ctx.enter_context(tc.tile_pool(name="nat", bufs=5))
+        nat_pool = ctx.enter_context(tc.tile_pool(name="nat", bufs=10))
         grouped_pool = ctx.enter_context(tc.tile_pool(name="grouped", bufs=2))
         keep = ctx.enter_context(tc.tile_pool(name="keep", bufs=1))
         sig_pool = ctx.enter_context(tc.tile_pool(name="sig", bufs=3))
         y_pool = ctx.enter_context(tc.tile_pool(name="y", bufs=2))
         out_pool = ctx.enter_context(tc.tile_pool(name="outs", bufs=4))
-        work = ctx.enter_context(tc.psum_pool(name="work", bufs=4))
-        gate_pool = ctx.enter_context(tc.psum_pool(name="gate", bufs=4))
+        for_scalar = ctx.enter_context(tc.psum_pool(name="for_scalar", bufs=4))
+        for_vector = ctx.enter_context(tc.psum_pool(name="for_vector", bufs=4))
 
         ident = const.tile([P, P], F32, name="ident")
         make_identity(nc, ident[:])
 
         def load(rows):
-            nat = nat_pool.tile([P, ROW_TILES, WIDTH], BF16, name="nat")
+            nat = nat_pool.tile([P, 2, WIDTH], BF16, name="nat")
             runs = rows.shape[1]
             nc.sync.dma_start(out=nat[:].rearrange("p (a b) k -> p a (b k)", a=runs), in_=rows)
             return nat
+
+        def load_block(rows):
+            return [load(rows[h]) for h in range(HALVES)]
 
         def mx_tiles(name):
             return {
@@ -66,15 +70,15 @@ def tile_aftfull_pb_kernel(tc, q, num, den, Wq, Wo, out):
                 "scales": keep.tile([P, PASSES * BLOCK], U8, name=name + "_scales", align_bytes=64),
             }
 
-        def turn(nat, c, pair):
+        def turn(nat, c, pool):
             words = nat[:].bitcast(F32)
-            bank = work.tile([P, 2, PAIR], F32, name="bank")
+            bank = pool.tile([P, 2, PAIR], F32, name="bank")
             for u in range(2):
-                for h in range(2):
+                for j in range(2):
                     block = 2 * c + u
                     nc.tensor.transpose(
-                        out=bank[:, u, h * P : (h + 1) * P],
-                        in_=words[:, 2 * pair + h, block * P : (block + 1) * P],
+                        out=bank[:, u, j * P : (j + 1) * P],
+                        in_=words[:, j, block * P : (block + 1) * P],
                         identity=ident[:],
                     )
             return bank
@@ -82,16 +86,22 @@ def tile_aftfull_pb_kernel(tc, q, num, den, Wq, Wo, out):
         def as_values(bank):
             return bank[:].bitcast(BF16).rearrange("p u (r e) -> p r u e", e=2)
 
-        def part_of(unit_tile, pair):
-            rows = unit_tile[:, pair * PAIR : (pair + 1) * PAIR, :]
+        def part_of(unit_tile, h):
+            rows = unit_tile[:, h * PAIR : (h + 1) * PAIR, :]
             return rows.rearrange("p r (u e) -> p r u e", e=2)
 
-        def regroup(nat, grouped, c, pair):
-            bank = turn(nat, c, pair)
-            nc.vector.tensor_copy(
-                out=grouped[:].bitcast(F32)[:, c, pair * PAIR : (pair + 1) * PAIR, :],
-                in_=bank[:].rearrange("p u r -> p r u"),
-            )
+        def new_grouped():
+            return grouped_pool.tile([P, PASSES, BLOCK, PACK], BF16, name="grouped", align_bytes=64)
+
+        def regroup(nat, grouped, h, on_scalar):
+            banks = [turn(nat, c, for_scalar if on_scalar else for_vector) for c in range(PASSES)]
+            for c in range(PASSES):
+                side_by_side = grouped[:].bitcast(F32)[:, c, h * PAIR : (h + 1) * PAIR, :]
+                planes = banks[c][:].rearrange("p u r -> p r u")
+                if on_scalar:
+                    nc.scalar.copy(out=side_by_side, in_=planes)
+                else:
+                    nc.vector.tensor_copy(out=side_by_side, in_=planes)
 
         def quantise(grouped, operand):
             nc.vector.quantize_mx(
@@ -100,21 +110,24 @@ def tile_aftfull_pb_kernel(tc, q, num, den, Wq, Wo, out):
                 in_=grouped[:].rearrange("p c r t -> p (c r t)"),
             )
 
-        def log_denominator(nat, n, g, pair):
-            bank = turn(nat, g, pair)
-            nc.scalar.activation(out=part_of(ratio[PASSES * n + g], pair), in_=as_values(bank), func=ACT.Ln)
+        def log_denominator(nat, n, h):
+            banks = [turn(nat, g, for_scalar) for g in range(PASSES)]
+            for g in range(PASSES):
+                nc.scalar.activation(
+                    out=part_of(ratio[PASSES * n + g], h), in_=as_values(banks[g]), func=ACT.Ln
+                )
 
         def ratio_unit(u):
             n, g = divmod(u, PASSES)
-            for pair in range(2):
-                bank = turn(num_nat[n], g, pair)
-                part = part_of(ratio[u], pair)
-                nc.vector.tensor_tensor(out=part, in0=as_values(bank), in1=part, op=MULT)
+            banks = [turn(num_nat[n][h], g, for_vector) for h in range(HALVES)]
+            for h in range(HALVES):
+                part = part_of(ratio[u], h)
+                nc.vector.tensor_tensor(out=part, in0=as_values(banks[h]), in1=part, op=MULT)
 
-        def mx_product(acc, stationary, s_col, moving, m_col):
+        def mx_product(acc, stationary, s_col, moving):
             for c in range(PASSES):
                 s_cols = slice(c * BLOCK + s_col, c * BLOCK + s_col + P)
-                m_cols = slice(c * BLOCK + m_col, c * BLOCK + m_col + BLOCK)
+                m_cols = slice(c * BLOCK, (c + 1) * BLOCK)
                 nc.tensor.matmul_mx(
                     out=acc[:],
                     lhsT=stationary["codes"][:, s_cols].bitcast(FP8X4),
@@ -129,8 +142,8 @@ def tile_aftfull_pb_kernel(tc, q, num, den, Wq, Wo, out):
             n, g = divmod(u, PASSES)
             sig = sig_pool.tile([P, PACK, BLOCK], F32, name="sig")
             for t in range(PACK):
-                acc = gate_pool.tile([P, BLOCK], F32, name="acc")
-                mx_product(acc, wq[g], t * P, qx[n], 0)
+                acc = for_scalar.tile([P, BLOCK], F32, name="bank")
+                mx_product(acc, wq[g], t * P, qx[n])
                 nc.scalar.activation(out=sig[:, t, :], in_=acc[:], func=ACT.Sigmoid)
             return sig
 
@@ -150,61 +163,80 @@ def tile_aftfull_pb_kernel(tc, q, num, den, Wq, Wo, out):
 
         def project(v):
             n, half = divmod(v, 2)
-            for i in (2 * half, 2 * half + 1):
+            first, second = 2 * half, 2 * half + 1
+            for i in (first, second):
                 result = out_pool.tile([P, WIDTH], F32, name="result")
                 for s in range(2):
-                    acc = work.tile([P, BLOCK], F32, name="bank")
-                    mx_product(acc, yx[n], i * P, wo[s], 0)
-                    cols = slice(s * BLOCK, (s + 1) * BLOCK)
-                    if i % 2 == 1 and s == 1:
-                        nc.vector.tensor_copy(out=result[:, cols], in_=acc[:])
-                    else:
-                        nc.scalar.copy(out=result[:, cols], in_=acc[:])
-                nc.sync.dma_start(out=out_rows[n][:, i, :], in_=result[:])
+                    acc = for_vector.tile([P, BLOCK], F32, name="bank")
+                    mx_product(acc, yx[n], i * P, wo[s])
+                    if i == first or s == 0:
+                        nc.scalar.copy(out=result[:, s * BLOCK : (s + 1) * BLOCK], in_=acc[:])
+                if i == first:
+                    nc.sync.dma_start(out=out_rows[n][:, i, :], in_=result[:])
+            return {"bank": acc, "result": result, "rows": out_rows[n][:, second, :]}
 
-        den_nat = {}
-        mx_nat = {}
-        mx_rows = [wq_rows[0], wq_rows[1]] + [q_rows[n] for n in range(CHUNKS)] + [wo_rows[0], wo_rows[1]]
+        def finish(left):
+            nc.vector.tensor_copy(out=left["result"][:, BLOCK:], in_=left["bank"][:])
+            nc.sync.dma_start(out=left["rows"], in_=left["result"][:])
+
+        first_rows = [wq_rows[0], wq_rows[1]] + [q_rows[n] for n in range(EARLY_CHUNKS)]
+        den_nat = []
+        first_nat = []
         for k in range(CHUNKS):
-            den_nat[k] = load(den_rows[k])
-            mx_nat[k] = load(mx_rows[k])
-        for k in range(CHUNKS, len(mx_rows)):
-            mx_nat[k] = load(mx_rows[k])
-        num_nat = [load(num_rows[n]) for n in range(CHUNKS)]
+            den_nat.append([])
+            first_nat.append([])
+            for h in range(HALVES):
+                den_nat[k].append(load(den_rows[k][h]))
+                first_nat[k].append(load(first_rows[k][h]))
+        wo_nat = [load_block(wo_rows[s]) for s in range(2)]
+        num_nat = [load_block(num_rows[n]) for n in range(CHUNKS)]
+        late_nat = [load_block(q_rows[n]) for n in range(EARLY_CHUNKS, CHUNKS)]
 
         wq = [mx_tiles("wq%d" % g) for g in range(PASSES)]
         qx = [mx_tiles("q%d" % n) for n in range(CHUNKS)]
         wo = [mx_tiles("wo%d" % s) for s in range(2)]
         yx = [mx_tiles("y%d" % n) for n in range(CHUNKS)]
-        operands = wq + qx + wo
         ratio = [keep.tile([P, BLOCK, PACK], F32, name="ratio%d" % u) for u in range(UNITS)]
 
-        grouped = {}
-        for k in range(len(operands)):
-            grouped[k] = grouped_pool.tile([P, PASSES, BLOCK, PACK], BF16, name="grouped", align_bytes=64)
-            for c in range(PASSES):
-                for pair in range(2):
-                    if k < CHUNKS:
-                        log_denominator(den_nat[k], k, c, pair)
-                    regroup(mx_nat[k], grouped[k], c, pair)
-            if k > 0:
-                quantise(grouped[k - 1], operands[k - 1])
-        quantise(grouped[len(operands) - 1], operands[len(operands) - 1])
+        early = wq + qx[:EARLY_CHUNKS] + wo
+        early_nat = first_nat + wo_nat
+        waiting = None
+        for k in range(len(early)):
+            grouped = new_grouped()
+            for h in range(HALVES):
+                if k < CHUNKS:
+                    log_denominator(den_nat[k][h], k, h)
+                regroup(early_nat[k][h], grouped, h, False)
+            if waiting is not None:
+                quantise(waiting, early[k - 1])
+            waiting = grouped
+        quantise(waiting, early[len(early) - 1])
         for u in range(UNITS):
             nc.scalar.activation(out=ratio[u][:], in_=ratio[u][:], func=ACT.Exp, scale=-1.0)
 
         sig = {0: gate(0)}
         y = {}
+        late_grouped = {}
         for u in range(RATIO_AHEAD):
             ratio_unit(u)
         for r in range(UNITS + PROJECT_BEHIND):
+            left = None
             if r >= PROJECT_BEHIND:
-                project(r - PROJECT_BEHIND)
+                left = project(r - PROJECT_BEHIND)
             if r + 1 < UNITS:
                 sig[r + 1] = gate(r + 1)
+            late, h = divmod(r, HALVES)
+            if late < CHUNKS - EARLY_CHUNKS:
+                if h == 0:
+                    late_grouped[late] = new_grouped()
+                regroup(late_nat[late][h], late_grouped[late], h, True)
             if 1 <= r <= UNITS:
                 quantise_y(r - 1, y[r - 1])
             if r < UNITS:
                 y[r] = blend(r, sig[r])
+            if left is not None:
+                finish(left)
+            if h == 0 and 1 <= late <= CHUNKS - EARLY_CHUNKS:
+                quantise(late_grouped[late - 1], qx[EARLY_CHUNKS + late - 1])
             if r + RATIO_AHEAD < UNITS:
                 ratio_unit(r + RATIO_AHEAD)

@@ -110,12 +110,10 @@ def tile_aftfull_pb_kernel(tc, q, num, den, Wq, Wo, out):
                 in_=grouped[:].rearrange("p c r t -> p (c r t)"),
             )
 
-        def log_denominator(nat, n, h):
+        def invert_denominator(nat, n, h):
             banks = [turn(nat, g, for_scalar) for g in range(PASSES)]
             for g in range(PASSES):
-                nc.scalar.activation(
-                    out=part_of(ratio[PASSES * n + g], h), in_=as_values(banks[g]), func=ACT.Ln
-                )
+                nc.vector.reciprocal(out=part_of(ratio[PASSES * n + g], h), in_=as_values(banks[g]))
 
         def ratio_unit(u):
             n, g = divmod(u, PASSES)
@@ -205,14 +203,12 @@ def tile_aftfull_pb_kernel(tc, q, num, den, Wq, Wo, out):
             grouped = new_grouped()
             for h in range(HALVES):
                 if k < CHUNKS:
-                    log_denominator(den_nat[k][h], k, h)
+                    invert_denominator(den_nat[k][h], k, h)
                 regroup(early_nat[k][h], grouped, h, False)
             if waiting is not None:
                 quantise(waiting, early[k - 1])
             waiting = grouped
         quantise(waiting, early[len(early) - 1])
-        for u in range(UNITS):
-            nc.scalar.activation(out=ratio[u][:], in_=ratio[u][:], func=ACT.Exp, scale=-1.0)
 
         sig = {0: gate(0)}
         y = {}

from contextlib import ExitStack

import concourse.mybir as mybir
from concourse.masks import make_identity

F32 = mybir.dt.float32
BF16 = mybir.dt.bfloat16
U32 = mybir.dt.uint32
U8 = mybir.dt.uint8
FP8X4 = mybir.dt.float8_e4m3fn_x4
ACT = mybir.ActivationFunctionType
MULT = mybir.AluOpType.mult

P = 128
PACK = 4
K_PASS = P * PACK
WIDTH = 1024
PASSES = WIDTH // K_PASS
BLOCK = 512
PAIR = 2 * P
HALVES = BLOCK // PAIR
TOKENS = 2048
CHUNKS = TOKENS // BLOCK
UNITS = CHUNKS * PASSES
EARLY_CHUNKS = 2
PROJECT_BEHIND = 3
RATIO_AHEAD = 7

FLOPS = 2 * 2 * TOKENS * WIDTH * WIDTH


def tile_aftfull_pb_kernel(tc, q, num, den, Wq, Wo, out):
    nc = tc.nc

    by_token = "(n p h j) k -> n h p (j k)"
    q_rows = q.flatten_outer_dims().rearrange(by_token, p=P, h=HALVES, j=2).unsqueeze(3)
    num_rows = num.flatten_outer_dims().rearrange(by_token, p=P, h=HALVES, j=2).unsqueeze(3)
    den_rows = den.flatten_outer_dims().rearrange(by_token, p=P, h=HALVES, j=2).unsqueeze(3)
    out_rows = out.flatten_outer_dims().rearrange("(n p i) o -> n p i o", p=P, i=2 * HALVES)
    wq_rows = Wq.rearrange("(g u p e) k -> g u p (e k)", u=HALVES, p=P, e=2).unsqueeze(3)
    wo_rows = Wo.rearrange("(s h j p) k -> s h p j k", h=HALVES, j=2, p=P)

    with ExitStack() as ctx:
        ctx.enter_context(tc.manual_schedule())
        const = ctx.enter_context(tc.tile_pool(name="const", bufs=1))
        nat_pool = ctx.enter_context(tc.tile_pool(name="nat", bufs=10))
        grouped_pool = ctx.enter_context(tc.tile_pool(name="grouped", bufs=2))
        keep = ctx.enter_context(tc.tile_pool(name="keep", bufs=1))
        sig_pool = ctx.enter_context(tc.tile_pool(name="sig", bufs=3))
        y_pool = ctx.enter_context(tc.tile_pool(name="y", bufs=2))
        out_pool = ctx.enter_context(tc.tile_pool(name="outs", bufs=4))
        for_scalar = ctx.enter_context(tc.psum_pool(name="for_scalar", bufs=4))
        for_vector = ctx.enter_context(tc.psum_pool(name="for_vector", bufs=4))

        ident = const.tile([P, P], F32, name="ident")
        make_identity(nc, ident[:])

        def load(rows):
            nat = nat_pool.tile([P, 2, WIDTH], BF16, name="nat")
            runs = rows.shape[1]
            nc.sync.dma_start(out=nat[:].rearrange("p (a b) k -> p a (b k)", a=runs), in_=rows)
            return nat

        def load_block(rows):
            return [load(rows[h]) for h in range(HALVES)]

        def mx_tiles(name):
            return {
                "codes": keep.tile([P, PASSES * BLOCK], U32, name=name + "_codes", align_bytes=64),
                "scales": keep.tile([P, PASSES * BLOCK], U8, name=name + "_scales", align_bytes=64),
            }

        def turn(nat, c, pool):
            words = nat[:].bitcast(F32)
            bank = pool.tile([P, 2, PAIR], F32, name="bank")
            for u in range(2):
                for j in range(2):
                    block = 2 * c + u
                    nc.tensor.transpose(
                        out=bank[:, u, j * P : (j + 1) * P],
                        in_=words[:, j, block * P : (block + 1) * P],
                        identity=ident[:],
                    )
            return bank

        def as_values(bank):
            return bank[:].bitcast(BF16).rearrange("p u (r e) -> p r u e", e=2)

        def part_of(unit_tile, h):
            rows = unit_tile[:, h * PAIR : (h + 1) * PAIR, :]
            return rows.rearrange("p r (u e) -> p r u e", e=2)

        def new_grouped():
            return grouped_pool.tile([P, PASSES, BLOCK, PACK], BF16, name="grouped", align_bytes=64)

        def regroup(nat, grouped, h, on_scalar):
            banks = [turn(nat, c, for_scalar if on_scalar else for_vector) for c in range(PASSES)]
            for c in range(PASSES):
                side_by_side = grouped[:].bitcast(F32)[:, c, h * PAIR : (h + 1) * PAIR, :]
                planes = banks[c][:].rearrange("p u r -> p r u")
                if on_scalar:
                    nc.scalar.copy(out=side_by_side, in_=planes)
                else:
                    nc.vector.tensor_copy(out=side_by_side, in_=planes)

        def quantise(grouped, operand):
            nc.vector.quantize_mx(
                out=operand["codes"][:].bitcast(FP8X4),
                scales=operand["scales"][:],
                in_=grouped[:].rearrange("p c r t -> p (c r t)"),
            )

        def invert_denominator(nat, n, h):
            banks = [turn(nat, g, for_scalar) for g in range(PASSES)]
            for g in range(PASSES):
                nc.vector.reciprocal(out=part_of(ratio[PASSES * n + g], h), in_=as_values(banks[g]))

        def ratio_unit(u):
            n, g = divmod(u, PASSES)
            banks = [turn(num_nat[n][h], g, for_vector) for h in range(HALVES)]
            for h in range(HALVES):
                part = part_of(ratio[u], h)
                nc.vector.tensor_tensor(out=part, in0=as_values(banks[h]), in1=part, op=MULT)

        def mx_product(acc, stationary, s_col, moving):
            for c in range(PASSES):
                s_cols = slice(c * BLOCK + s_col, c * BLOCK + s_col + P)
                m_cols = slice(c * BLOCK, (c + 1) * BLOCK)
                nc.tensor.matmul_mx(
                    out=acc[:],
                    lhsT=stationary["codes"][:, s_cols].bitcast(FP8X4),
                    lhsT_scale=stationary["scales"][:, s_cols],
                    rhs=moving["codes"][:, m_cols].bitcast(FP8X4),
                    rhs_scale=moving["scales"][:, m_cols],
                    start=(c == 0),
                    stop=(c == PASSES - 1),
                )

        def gate(u):
            n, g = divmod(u, PASSES)
            sig = sig_pool.tile([P, PACK, BLOCK], F32, name="sig")
            for t in range(PACK):
                acc = for_scalar.tile([P, BLOCK], F32, name="bank")
                mx_product(acc, wq[g], t * P, qx[n])
                nc.scalar.activation(out=sig[:, t, :], in_=acc[:], func=ACT.Sigmoid)
            return sig

        def blend(u, sig):
            y = y_pool.tile([P, BLOCK, PACK], BF16, name="y", align_bytes=64)
            nc.vector.tensor_tensor(out=y[:], in0=sig[:].rearrange("p t r -> p r t"), in1=ratio[u][:], op=MULT)
            return y

        def quantise_y(u, y):
            n, g = divmod(u, PASSES)
            cols = slice(g * BLOCK, (g + 1) * BLOCK)
            nc.vector.quantize_mx(
                out=yx[n]["codes"][:, cols].bitcast(FP8X4),
                scales=yx[n]["scales"][:, cols],
                in_=y[:].rearrange("p r t -> p (r t)"),
            )

        def project(v):
            n, half = divmod(v, 2)
            first, second = 2 * half, 2 * half + 1
            for i in (first, second):
                result = out_pool.tile([P, WIDTH], F32, name="result")
                for s in range(2):
                    acc = for_vector.tile([P, BLOCK], F32, name="bank")
                    mx_product(acc, yx[n], i * P, wo[s])
                    if i == first or s == 0:
                        nc.scalar.copy(out=result[:, s * BLOCK : (s + 1) * BLOCK], in_=acc[:])
                if i == first:
                    nc.sync.dma_start(out=out_rows[n][:, i, :], in_=result[:])
            return {"bank": acc, "result": result, "rows": out_rows[n][:, second, :]}

        def finish(left):
            nc.vector.tensor_copy(out=left["result"][:, BLOCK:], in_=left["bank"][:])
            nc.sync.dma_start(out=left["rows"], in_=left["result"][:])

        first_rows = [wq_rows[0], wq_rows[1]] + [q_rows[n] for n in range(EARLY_CHUNKS)]
        den_nat = []
        first_nat = []
        for k in range(CHUNKS):
            den_nat.append([])
            first_nat.append([])
            for h in range(HALVES):
                den_nat[k].append(load(den_rows[k][h]))
                first_nat[k].append(load(first_rows[k][h]))
        wo_nat = [load_block(wo_rows[s]) for s in range(2)]
        num_nat = [load_block(num_rows[n]) for n in range(CHUNKS)]
        late_nat = [load_block(q_rows[n]) for n in range(EARLY_CHUNKS, CHUNKS)]

        wq = [mx_tiles("wq%d" % g) for g in range(PASSES)]
        qx = [mx_tiles("q%d" % n) for n in range(CHUNKS)]
        wo = [mx_tiles("wo%d" % s) for s in range(2)]
        yx = [mx_tiles("y%d" % n) for n in range(CHUNKS)]
        ratio = [keep.tile([P, BLOCK, PACK], F32, name="ratio%d" % u) for u in range(UNITS)]

        early = wq + qx[:EARLY_CHUNKS] + wo
        early_nat = first_nat + wo_nat
        waiting = None
        for k in range(len(early)):
            grouped = new_grouped()
            for h in range(HALVES):
                if k < CHUNKS:
                    invert_denominator(den_nat[k][h], k, h)
                regroup(early_nat[k][h], grouped, h, False)
            if waiting is not None:
                quantise(waiting, early[k - 1])
            waiting = grouped
        quantise(waiting, early[len(early) - 1])

        sig = {0: gate(0)}
        y = {}
        late_grouped = {}
        for u in range(RATIO_AHEAD):
            ratio_unit(u)
        for r in range(UNITS + PROJECT_BEHIND):
            left = None
            if r >= PROJECT_BEHIND:
                left = project(r - PROJECT_BEHIND)
            if r + 1 < UNITS:
                sig[r + 1] = gate(r + 1)
            late, h = divmod(r, HALVES)
            if late < CHUNKS - EARLY_CHUNKS:
                if h == 0:
                    late_grouped[late] = new_grouped()
                regroup(late_nat[late][h], late_grouped[late], h, True)
            if 1 <= r <= UNITS:
                quantise_y(r - 1, y[r - 1])
            if r < UNITS:
                y[r] = blend(r, sig[r])
            if left is not None:
                finish(left)
            if h == 0 and 1 <= late <= CHUNKS - EARLY_CHUNKS:
                quantise(late_grouped[late - 1], qx[EARLY_CHUNKS + late - 1])
            if r + RATIO_AHEAD < UNITS:
                ratio_unit(r + RATIO_AHEAD)
